import numpy as np
import ml_dtypes


def mxq(x, axis, fmt="e4m3"):
    dtype, down = {"e4m3": (ml_dtypes.float8_e4m3fn, 7), "e5m2": (ml_dtypes.float8_e5m2, 14)}[fmt]
    v = np.moveaxis(np.asarray(x, np.float32).astype(ml_dtypes.bfloat16).astype(np.float64), axis, -1)
    blocks = v.reshape(v.shape[:-1] + (-1, 32))
    amax = np.abs(blocks).max(-1, keepdims=True)
    byte = np.maximum(np.where(amax > 0, np.frexp(amax)[1] - 1 + 127, 0) - down, 1)
    scale = np.exp2(byte - 127.0)
    codes = (blocks / scale).astype(np.float32).astype(dtype).astype(np.float64)
    return np.moveaxis((codes * scale).reshape(v.shape), -1, axis)


WIDE = False


def mx_kscale(k):
    if not WIDE:
        return np.ones(k)
    levels = np.array([10, -10, 5, -5, 0])
    if k % 512:
        return np.exp2(np.random.permutation(np.resize(levels, k // 32))).repeat(32)
    a = np.empty((k // 512, 16))
    for p in range(k // 512):
        a[p, :8] = np.random.permutation(np.resize(levels, 8))
        for g in range(8):
            far = levels[np.abs(levels - a[p, g]) >= 10]
            a[p, g + 8] = far[np.random.randint(len(far))]
    return np.exp2(a.ravel()).repeat(32)


BF16 = ml_dtypes.bfloat16


def bf(x):
    return np.asarray(x, np.float32).astype(BF16)


def f64(x):
    return np.asarray(x).astype(np.float64)


B, S, D, H, DN, DR, DV, QL, KVL, LBLK = 4, 2048, 512, 4, 32, 32, 128, 512, 512, 64
DQ = DN + DR


def silu(v):
    return v / (1.0 + np.exp(-v))


def apply_rope(x, fc):
    xr, xi = x[..., 0::2], x[..., 1::2]
    cos = fc[None, :, None, :, 0]
    sin = fc[None, :, None, :, 1]
    yr = xr * cos - xi * sin
    yi = xr * sin + xi * cos
    return np.stack([yr, yi], axis=-1).reshape(x.shape)


def eta(t):
    m = t.reshape(t.shape[0], H, -1).max(-1)
    m = np.where(m == 0, 1e-6, m)
    return np.minimum(10.0 / m, 1.0)


def draw0():
    s, t = mx_kscale(D), mx_kscale(QL)
    amp = np.linspace(0.5, 1.5, S)[None, :, None]
    ang = np.arange(S)[:, None] / 10000.0 ** (np.arange(0, DR, 2) / DR)[None, :]
    return {"x": bf(np.random.standard_normal((B, S, D)) * amp * s),
            "freqs_cis": bf(np.stack([np.cos(ang), np.sin(ang)], axis=-1)),
            "wq_a": bf(np.random.standard_normal((QL, D)) / np.sqrt(D) / s[None, :] * t[:, None]),
            "wq_b": bf(np.random.standard_normal((H * DQ, QL)) * 2.5 / np.sqrt(QL) / t[None, :])}


def core(x, freqs_cis, wq_a, wq_b):
    q_c = mxq(f64(x), 2, "e4m3") @ mxq(f64(wq_a), 1, "e4m3").T
    q = (mxq(q_c, 2, "e4m3") @ mxq(f64(wq_b), 1, "e4m3").T).reshape(B, S, H, DQ)
    q_nope, q_pe = q[..., :DN], q[..., DN:]
    q_pe = apply_rope(q_pe, f64(freqs_cis))
    q_nope = silu(q_nope)
    q_pe = silu(q_pe)
    return q_nope * eta(q_nope)[:, None, :, None], q_pe * eta(q_pe)[:, None, :, None]


def e4m3fn_bytes(y):
    return np.clip(np.asarray(y, np.float64), -448.0, 448.0).astype(np.float32).astype(ml_dtypes.float8_e4m3fn).view(np.uint8)


def e4m3fn_values(b):
    return np.asarray(b, np.uint8).view(ml_dtypes.float8_e4m3fn).astype(np.float64)


def setup_inputs():
    d = draw0()
    x0 = np.asarray(d['x']).astype(np.float64)
    s = (np.max(np.abs(x0), axis=(0, 1), keepdims=True) / 448.0).astype(np.float32)
    out = {}
    for k, v in d.items():
        if k == 'x':
            out['x_bytes'] = e4m3fn_bytes(x0 / s.astype(np.float64))
            out['x_scale'] = s
        else:
            out[k] = v
    return out


def reference(x_bytes, x_scale, freqs_cis, wq_a, wq_b):
    return core(e4m3fn_values(x_bytes) * x_scale.astype(np.float64), freqs_cis, wq_a, wq_b)

@@ -1,0 +1,489 @@
+from contextlib import ExitStack
+
+import concourse.mybir as mybir
+from concourse.masks import make_identity
+
+B, S, D, H = 4, 2048, 512, 4
+FLOPS = 2 * B * S * D * (512 + 256)
+
+F32 = mybir.dt.float32
+BF16 = mybir.dt.bfloat16
+U32 = mybir.dt.uint32
+U8 = mybir.dt.uint8
+FP8 = mybir.dt.float8_e4m3fn
+FP8X4 = mybir.dt.float8_e4m3fn_x4
+ALU = mybir.AluOpType
+ACT = mybir.ActivationFunctionType
+AXIS_X = mybir.AxisListType.X
+
+P = 128
+G = 4
+J = 4
+CHUNKS = B * G
+G_CLAMP = False
+G_ROPE = False
+E2 = "SVSVSSSS"
+E3 = "VSVVSS"
+TABLE_STEPS = [2, 4, 5, 6]
+UNITS = [(0, 0, 2), (0, 2, 2)] + [(c, 0, J) for c in range(1, CHUNKS - 1)] + [(CHUNKS - 1, 0, 2), (CHUNKS - 1, 2, 2)]
+
+
+def tile_ssa_pa_t_kernel(tc, x_bytes, x_scale, freqs_cis, wq_a, wq_b, out_0, out_1):
+    nc = tc.nc
+    outs = (out_0, out_1)
+
+    with ExitStack() as ctx:
+        keep = ctx.enter_context(tc.tile_pool(name="keep", bufs=1))
+        work = ctx.enter_context(tc.tile_pool(name="work", bufs=3))
+        psum = ctx.enter_context(tc.psum_pool(name="psum", bufs=1))
+        ctx.enter_context(tc.manual_schedule())
+
+        def bank(tag, bufs):
+            return psum.tile([P, 512], F32, name=tag, tag=tag, bufs=bufs)
+
+        scale_col = keep.tile([P, 4], F32)
+        nc.sync.dma_start(out=scale_col[:], in_=x_scale.rearrange("a b (p t) -> p (a b t)", t=4))
+        x_raw = []
+
+        def load_x(c):
+            t = keep.tile([P, J * D], U8, name="x_raw%d" % c, align_bytes=64)
+            src = x_bytes[c // G].rearrange("(g p j) k -> g p (j k)", p=P, j=J)[c % G]
+            nc.sync.dma_start(out=t[:], in_=src)
+            x_raw.append(t)
+
+        load_x(0)
+        freq_raw = keep.tile([P, G, J * 32], BF16)
+        nc.sync.dma_start(out=freq_raw[:], in_=freqs_cis.rearrange("(g p j) a e -> p g (j a e)", p=P, j=J))
+        wa_raw = keep.tile([P, 4 * D], BF16)
+        nc.sync.dma_start(out=wa_raw[:], in_=wq_a.rearrange("(m t) k -> m (t k)", t=4))
+        load_x(1)
+        wb_raw = keep.tile([P, 2 * D], BF16)
+        nc.sync.dma_start(out=wb_raw[:], in_=wq_b.rearrange("(m e) k -> m (e k)", e=2))
+        for c in range(2, CHUNKS):
+            load_x(c)
+
+        ident = keep.tile([P, P], F32)
+        make_identity(nc, ident[:])
+        warm = keep.tile([P, 1], F32)
+        nc.scalar.activation(out=warm[:], in_=ident[:, 0:1], func=ACT.Silu)
+        sign = keep.tile([P, 1], F32)
+        nc.gpsimd.memset(sign[0:64, :], -1.0)
+        nc.gpsimd.memset(sign[64:128, :], 1.0)
+        stats = keep.tile([P, P], F32)
+        nc.gpsimd.memset(stats[:], 0.0)
+
+        def turn_words(dst_bank, src_bf16):
+            words = src_bf16.bitcast(F32)
+            for j in range(2):
+                for u in range(2):
+                    q = 2 * j + u
+                    nc.tensor.transpose(dst_bank[:, q * P:(q + 1) * P],
+                                        words[:, 256 * j + u:256 * (j + 1):2], ident[:])
+
+        def interleave_words(dst_bf16, src_bank):
+            nc.scalar.copy(out=dst_bf16.bitcast(F32).rearrange("p (j r u) -> p j r u", j=2, u=2),
+                           in_=src_bank[:].rearrange("p (j u r) -> p j r u", j=2, u=2))
+
+        scale_row = keep.tile([P, 2 * D], F32)
+        sb = bank("n", 1)
+        for t in range(4):
+            nc.tensor.transpose(sb[:, t * P:(t + 1) * P], scale_col[:, t:t + 1].to_broadcast([P, P]), ident[:])
+        nc.vector.tensor_copy(out=scale_row[:, 0:D].rearrange("p (n t) -> p n t", t=4),
+                              in_=sb[:].rearrange("p (t n) -> p n t", t=4))
+        nc.scalar.copy(out=scale_row[:, D:2 * D], in_=scale_row[:, 0:D])
+
+        wa_codes = keep.tile([P, 512], U32, align_bytes=64)
+        wa_scales = keep.tile([P, 512], U8, align_bytes=64)
+        wa_grouped = keep.tile([P, 2048], BF16, align_bytes=64)
+        wn_codes = keep.tile([P, 128], U32, align_bytes=64)
+        wn_scales = keep.tile([P, 128], U8, align_bytes=64)
+        wn_grouped = keep.tile([P, 512], BF16, align_bytes=64)
+        wp_codes = keep.tile([P, 256], U32, align_bytes=64)
+        wp_scales = keep.tile([P, 256], U8, align_bytes=64)
+        wp_grouped = keep.tile([P, 1024], BF16, align_bytes=64)
+
+        st = {}
+
+        def halves(u):
+            return range(UNITS[u][1] // 2, (UNITS[u][1] + UNITS[u][2]) // 2)
+
+        def widen(u, half):
+            c = UNITS[u][0]
+            t = work.tile([P, 2 * D], BF16, name="x_wide", tag="x_wide", bufs=4, align_bytes=64)
+            st["xw", c, half] = t
+            src = x_raw[c][:, half * 2 * D:(half + 1) * 2 * D].bitcast(FP8)
+            if u == 0:
+                for j in range(2):
+                    nc.vector.tensor_tensor(out=t[:, j * D:(j + 1) * D], in0=src[:, j * D:(j + 1) * D],
+                                            in1=scale_row[:, 0:D], op=ALU.mult)
+            else:
+                nc.vector.tensor_tensor(out=t[:], in0=src, in1=scale_row[:], op=ALU.mult)
+
+        def turn_x(u):
+            c = UNITS[u][0]
+            for half in halves(u):
+                b = bank("xt", 2)
+                st["xt", c, half] = b
+                turn_words(b, st["xw", c, half][:])
+
+        def grouprevx(u):
+            c = UNITS[u][0]
+            t = work.tile([P, 2048], BF16, name="x_grouped", tag="x_grouped", bufs=2, align_bytes=64)
+            st["xg", u] = t
+            for i, half in enumerate(halves(u)):
+                interleave_words(t[:, i * 1024:(i + 1) * 1024], st["xt", c, half])
+
+        def quantize(kind, u):
+            n = UNITS[u][2] * P
+            codes = work.tile([P, 512], U32, name=kind + "_codes", tag=kind + "_codes", bufs=3, align_bytes=64)
+            scales = work.tile([P, 512], U8, name=kind + "_scales", tag=kind + "_scales", bufs=3, align_bytes=64)
+            st[kind + "q", u] = (codes, scales)
+            nc.vector.quantize_mx(out=codes[:, 0:n].bitcast(FP8X4), scales=scales[:, 0:n],
+                                  in_=st[kind + "g", u][:, 0:4 * n])
+
+        def mx(out, lhs, lcols, rhs, rcols):
+            nc.tensor.matmul_mx(out=out, lhsT=lhs[0][:, lcols].bitcast(FP8X4), lhsT_scale=lhs[1][:, lcols],
+                                rhs=rhs[0][:, rcols].bitcast(FP8X4), rhs_scale=rhs[1][:, rcols],
+                                start=True, stop=True)
+
+        def down(u, j):
+            if j >= UNITS[u][2]:
+                return
+            b = bank("qc", 2)
+            st["qcb", u, j] = b
+            for t in range(4):
+                cols = slice(t * P, (t + 1) * P)
+                mx(b[:, cols], (wa_codes, wa_scales), cols, st["xq", u], slice(j * P, (j + 1) * P))
+
+        def grouprevq(u, j):
+            if j >= UNITS[u][2]:
+                return
+            if j == 0:
+                st["qg", u] = work.tile([P, 2048], BF16, name="q_grouped", tag="q_grouped", bufs=2, align_bytes=64)
+            nc.scalar.copy(out=st["qg", u][:, j * 512:(j + 1) * 512].rearrange("p (n t) -> p n t", t=4),
+                           in_=st["qcb", u, j][:].rearrange("p (t n) -> p n t", t=4))
+
+        def up(u):
+            n = UNITS[u][2] * P
+            for r in range(2):
+                if r == 0 or n == 512:
+                    b = bank("pp", 2)
+                lo = 0 if n == 512 else r * n
+                st["pp", u, r] = b[:, lo:lo + n]
+                mx(st["pp", u, r], (wp_codes, wp_scales), slice(64 * r, 64 * r + P), st["qq", u], slice(0, n))
+            b = bank("xt", 2) if u == len(UNITS) - 1 else bank("n", 1)
+            st["n", u] = b
+            for j in range(UNITS[u][2]):
+                cols = slice(j * P, (j + 1) * P)
+                mx(b[:, cols], st["qq", u], cols, (wn_codes, wn_scales), slice(0, P))
+
+        def res_of(u, a):
+            c, j0, nj = UNITS[u]
+            if ("res", c // G) not in st:
+                st["res", c // G] = work.tile([P, G * 1024], F32, name="res", tag="res", bufs=3)
+            lo = (c % G) * 1024 + a * 512 + j0 * P
+            return st["res", c // G][:, lo:lo + nj * P]
+
+        def silu_n(u):
+            n = UNITS[u][2] * P
+            nc.scalar.activation(out=res_of(u, 0), in_=st["n", u][:, 0:n], func=ACT.Silu)
+
+        def rope_table(u):
+            c, j0, nj = UNITS[u]
+            return st["tab", c % G][:, j0 * P:(j0 + nj) * P].bitcast(BF16).rearrange("p (n e) -> p n e", e=2)
+
+        def rope_a(u):
+            n = UNITS[u][2] * P
+            ta = work.tile([P, 512], F32, name="rope_a", tag="rope_a", bufs=2)
+            st["ra", u] = ta
+            nc.vector.tensor_tensor(out=ta[:, 0:n], in0=st["pp", u, 0], in1=rope_table(u)[:, :, 0], op=ALU.mult)
+
+        def rope_b(u):
+            n = UNITS[u][2] * P
+            tb = work.tile([P, 512], F32, name="rope_b", tag="rope_b", bufs=2)
+            st["rb", u] = tb
+            if G_ROPE and u < len(UNITS) - 2:
+                tcopy = work.tile([P, 512], F32, name="rope_c", tag="rope_c", bufs=2)
+                nc.scalar.activation(out=tcopy[:, 0:n], in_=st["pp", u, 1], func=ACT.Copy, scale=sign[:])
+                nc.gpsimd.tensor_tensor(out=tb[:, 0:n], in0=tcopy[:, 0:n], in1=rope_table(u)[:, :, 1], op=ALU.mult)
+            else:
+                nc.vector.scalar_tensor_tensor(out=tb[:, 0:n], in0=st["pp", u, 1], scalar=sign[:],
+                                               in1=rope_table(u)[:, :, 1], op0=ALU.mult, op1=ALU.mult)
+
+        def turn_p(u):
+            b = bank("qc", 2) if u == len(UNITS) - 1 else bank("r", 1)
+            st["r", u] = b
+            for j in range(UNITS[u][2]):
+                cols = slice(j * P, (j + 1) * P)
+                for i, k in enumerate(("ra", "rb")):
+                    nc.tensor.matmul(out=b[:, cols], lhsT=st[k, u][:, cols], rhs=ident[:],
+                                     is_transpose=True, start=(i == 0), stop=(i == 1))
+
+        def silu_p(u):
+            nj = UNITS[u][2]
+            nc.scalar.activation(
+                out=res_of(u, 1).rearrange("p (j f e) -> p j f e", j=nj, e=2),
+                in_=st["r", u][:, 0:nj * P].rearrange("p (j e f) -> p j f e", j=nj, e=2), func=ACT.Silu)
+
+        def row_max(c):
+            g = c % G
+            nc.vector.tensor_reduce(
+                out=stats[:, 2 * c:2 * c + 2],
+                in_=st["res", c // G][:, g * 1024:(g + 1) * 1024].rearrange("p (a n) -> p a n", a=2),
+                axis=AXIS_X, op=ALU.max)
+
+        def eta_math(e, w, i):
+            if i == 1:
+                nc.vector.scalar_tensor_tensor(out=e[:, w:2 * w], in0=e[:, 0:w], scalar=0.0, in1=e[:, 0:w],
+                                               op0=ALU.is_equal, op1=ALU.add)
+            elif i == 2:
+                nc.vector.reciprocal(out=e[:, 2 * w:3 * w], in_=e[:, w:2 * w])
+            else:
+                nc.vector.tensor_scalar(out=e[:, 3 * w:4 * w], in0=e[:, 2 * w:3 * w], scalar1=10.0, scalar2=1.0,
+                                        op0=ALU.mult, op1=ALU.min)
+
+        def eta_turn(b):
+            t = bank("n", 1)
+            st["eb", b] = t
+            nc.tensor.transpose(t[:, 0:P], stats[:], ident[:])
+
+        def eta_step(b, i):
+            if i == 0:
+                st["e", b] = work.tile([P, 4], F32, name="eta_col", tag="eta_col", bufs=2)
+                nc.vector.tensor_reduce(out=st["e", b][:, 0:1], in_=st["eb", b][:, 0:P], axis=AXIS_X, op=ALU.max)
+            else:
+                eta_math(st["e", b], 1, i)
+
+        def eta_spread(b):
+            t = bank("n", 1)
+            st["es", b] = t
+            nc.tensor.transpose(t[:, 0:P], st["e", b][:, 3:4].to_broadcast([P, P]), ident[:])
+
+        def eta_copy(b):
+            t = work.tile([P, 8], F32, name="eta_row", tag="eta_row", bufs=2)
+            st["eta", b] = t
+            nc.scalar.copy(out=t[:], in_=st["es", b][:, 8 * b:8 * b + 8])
+
+        def clamp(b, a, h, eng, gs=slice(0, G), col=None):
+            v = st["res", b][:].rearrange("p (g a j h d) -> p a h g j d", g=G, a=2, j=J, h=H)[:, a, h, gs]
+            if col is None:
+                col = st["eta", b][:, 2 * h + a:2 * h + a + 1]
+            if eng == "V":
+                nc.vector.tensor_scalar(out=v, in0=v, scalar1=col, scalar2=None, op0=ALU.mult)
+            elif eng == "G":
+                nc.gpsimd.tensor_scalar(out=v, in0=v, scalar1=col, scalar2=0.0, op0=ALU.mult, op1=ALU.add)
+            else:
+                nc.scalar.activation(out=v, in_=v, func=ACT.Copy, scale=col)
+
+        def store(b, a, gs=slice(0, G)):
+            src = st["res", b][:].rearrange("p (g a n) -> p a g n", g=G, a=2)[:, a, gs]
+            dst = outs[a][b].rearrange("(g p j) h d -> p g (j h d)", p=P, j=J)[:, gs]
+            nc.sync.dma_start(out=dst, in_=src)
+
+        def table_spread(g):
+            t = work.tile([P, 512], F32, name="freq_rep", tag="freq_rep", bufs=2)
+            st["frep", g] = t
+            words = freq_raw[:, g, :].bitcast(F32).rearrange("p (j a) -> p j a", j=J)
+            nc.scalar.copy(out=t[:].rearrange("p (j r a) -> p j r a", j=J, r=8),
+                           in_=words.unsqueeze(2).broadcast_to([P, J, 8, 16]))
+
+        def table_turn(g):
+            b = bank("n", 1)
+            st["tb", g] = b
+            for j in range(J):
+                cols = slice(j * P, (j + 1) * P)
+                nc.tensor.transpose(b[:, cols], st["frep", g][:, cols], ident[:])
+
+        def table_copy(g):
+            t = keep.tile([P, 512], F32, name="table%d" % g)
+            st["tab", g] = t
+            nc.scalar.copy(out=t[:], in_=st["tb", g][:])
+
+        NU = len(UNITS)
+        last = B - 1
+
+        def live(u):
+            return 0 <= u < NU
+
+        tail_stats = keep.tile([P, 2], F32)
+        tail_eta = keep.tile([P, 8], F32)
+
+        def tail_max(a):
+            lo = (G - 1) * 1024 + a * 512
+            nc.vector.tensor_reduce(out=tail_stats[:, a:a + 1], in_=st["res", last][:, lo:lo + 512],
+                                    axis=AXIS_X, op=ALU.max)
+
+        def tail_turn(a):
+            t = bank("xt", 2)
+            st["tt", a] = t
+            nc.tensor.transpose(t[:, 0:P], tail_stats[:, a:a + 1].to_broadcast([P, P]), ident[:])
+
+        def tail_step(a, i):
+            e = tail_eta[:, 4 * a:4 * a + 4]
+            if i == 0:
+                nc.vector.tensor_reduce(out=e[:, 0:1], in_=st["tt", a][:, 0:P], axis=AXIS_X, op=ALU.max)
+            else:
+                eta_math(e, 1, i)
+
+        def clamp_n(b, i, eng):
+            a, h = divmod(i, H)
+            clamp(b, a, h, eng)
+            if h == H - 1:
+                store(b, a)
+
+        def clamp_slot(s, slot):
+            b, i = divmod(s - 10, G)
+            if s >= 10 and b < 2:
+                clamp_n(b, 2 * i + slot, "G" if G_CLAMP else "S")
+            if s == NU:
+                for i in range(2):
+                    clamp_n(2, 2 * slot + i, "G" if G_CLAMP else E2[2 * slot + i])
+
+        for s in range(NU + 1):
+            eb, ei = divmod(s - 9, G)
+            eta_a = s >= 9 and ei == 0 and eb < last
+            eta_b = s >= 9 and ei == 1 and eb < last
+            if live(s - 3):
+                quantize("q", s - 3)
+            if live(s - 1):
+                turn_x(s - 1)
+            if live(s - 4):
+                turn_p(s - 4)
+            if s == 1:
+                wab = [bank("pp", 2), bank("pp", 2)]
+                for i in range(2):
+                    turn_words(wab[i], wa_raw[:, i * 1024:(i + 1) * 1024])
+            if s == 2:
+                wbb = bank("r", 1)
+                turn_words(wbb, wb_raw[:])
+            if s in TABLE_STEPS:
+                table_turn(TABLE_STEPS.index(s))
+            if eta_a:
+                eta_turn(eb)
+            if eta_b:
+                eta_spread(eb)
+            if live(s - 1):
+                grouprevx(s - 1)
+            if live(s):
+                widen(s, halves(s)[0])
+            if eta_a:
+                eta_step(eb, 0)
+            if eta_b:
+                eta_copy(eb)
+            if s == 1:
+                for i in range(2):
+                    interleave_words(wa_grouped[:, i * 1024:(i + 1) * 1024], wab[i])
+            if s == 2:
+                src = wbb[:].rearrange("p (e u h f j) -> p f h j e u", e=2, u=2, h=H, f=2)
+                nc.scalar.copy(out=wn_grouped[:].bitcast(F32).rearrange("p (h j e u) -> p h j e u", h=H, e=2, u=2),
+                               in_=src[:, 0])
+                srcp = wbb[:].rearrange("p (e u h f j) -> p f e h j u", e=2, u=2, h=H, f=2)
+                for r in range(2):
+                    nc.scalar.copy(
+                        out=wp_grouped[:, r * 512:(r + 1) * 512].bitcast(F32).rearrange(
+                            "p (e h j u) -> p e h j u", e=2, h=H, u=2),
+                        in_=srcp[:, 1])
+            if s in TABLE_STEPS:
+                table_copy(TABLE_STEPS.index(s))
+            clamp_slot(s, 0)
+            if live(s - 4):
+                silu_p(s - 4)
+            if live(s - 1):
+                quantize("x", s - 1)
+            if eta_a:
+                eta_step(eb, 1)
+            if live(s - 2):
+                down(s - 2, 0)
+                down(s - 2, 1)
+            if live(s - 3):
+                up(s - 3)
+            if live(s - 2):
+                grouprevq(s - 2, 0)
+                grouprevq(s - 2, 1)
+            if live(s) and len(halves(s)) > 1:
+                widen(s, halves(s)[1])
+            if eta_a:
+                eta_step(eb, 2)
+            if live(s - 3):
+                silu_n(s - 3)
+            if live(s - 2):
+                down(s - 2, 2)
+                down(s - 2, 3)
+            if live(s - 3):
+                rope_a(s - 3)
+                rope_b(s - 3)
+            if eta_a:
+                eta_step(eb, 3)
+            if s == 1:
+                nc.vector.quantize_mx(out=wa_codes[:].bitcast(FP8X4), scales=wa_scales[:], in_=wa_grouped[:])
+            if s == 2:
+                nc.vector.quantize_mx(out=wn_codes[:].bitcast(FP8X4), scales=wn_scales[:], in_=wn_grouped[:])
+                nc.vector.quantize_mx(out=wp_codes[:].bitcast(FP8X4), scales=wp_scales[:], in_=wp_grouped[:])
+            if live(s - 2):
+                grouprevq(s - 2, 2)
+                grouprevq(s - 2, 3)
+            if 1 <= s - 4 < NU - 2:
+                row_max(UNITS[s - 4][0])
+            clamp_slot(s, 1)
+            if s + 1 in TABLE_STEPS:
+                table_spread(TABLE_STEPS.index(s + 1))
+
+        uprev, ua, ub = NU - 3, NU - 2, NU - 1
+        e2 = "GGGGGGGG" if G_CLAMP else E2
+        e3 = "GGGGGG" if G_CLAMP else E3
+        turn_p(uprev)
+        down(ub, 0)
+        down(ub, 1)
+        quantize("q", ua)
+        silu_p(uprev)
+        grouprevq(ub, 0)
+        grouprevq(ub, 1)
+        up(ua)
+        clamp_n(2, 4, e2[4])
+        clamp_n(2, 5, e2[5])
+        row_max(CHUNKS - 2)
+        eta_turn_at = bank("r", 1)
+        nc.tensor.transpose(eta_turn_at[:, 0:P], stats[:], ident[:])
+        st["eb", last] = eta_turn_at
+        quantize("q", ub)
+        up(ub)
+        silu_n(ua)
+        silu_n(ub)
+        eta_step(last, 0)
+        rope_a(ua)
+        eta_step(last, 1)
+        rope_b(ua)
+        eta_step(last, 2)
+        turn_p(ua)
+        rope_a(ub)
+        eta_step(last, 3)
+        rope_b(ub)
+        eta_spread(last)
+        turn_p(ub)
+        clamp_n(2, 6, e2[6])
+        clamp_n(2, 7, e2[7])
+        tail_max(0)
+        tail_turn(0)
+        silu_p(ua)
+        eta_copy(last)
+        silu_p(ub)
+        tail_step(0, 0)
+        clamp(last, 0, 0, e3[0])
+        tail_step(0, 1)
+        clamp(last, 0, 1, e3[1])
+        tail_max(1)
+        tail_turn(1)
+        tail_step(0, 2)
+        clamp(last, 0, 2, e3[2])
+        tail_step(0, 3)
+        tail_step(1, 0)
+        clamp(last, 0, 3, "V", col=tail_eta[:, 3:4])
+        store(last, 0)
+        tail_step(1, 1)
+        clamp(last, 1, 0, e3[3])
+        tail_step(1, 2)
+        clamp(last, 1, 1, e3[4])
+        tail_step(1, 3)
+        clamp(last, 1, 2, e3[5])
+        clamp(last, 1, 3, "V", col=tail_eta[:, 7:8])
+        store(last, 1)

@@ -22,9 +22,10 @@ J = 4
 CHUNKS = B * G
 G_CLAMP = False
 G_ROPE = False
-E2 = "SVSVSSSS"
-E3 = "VSVVSS"
-TABLE_STEPS = [2, 4, 5, 6]
+E2 = "VVVVSSVS"
+E3 = "SVSSSS"
+WIDEN = {0: (0, 1), 1: (0, 1), 7: (0,), 8: (0,), 16: (0,), 17: (0,)}
+TABLE_STEPS = [3, 5, 6, 7]
 UNITS = [(0, 0, 2), (0, 2, 2)] + [(c, 0, J) for c in range(1, CHUNKS - 1)] + [(CHUNKS - 1, 0, 2), (CHUNKS - 1, 2, 2)]
 
 
@@ -62,6 +63,7 @@ def tile_ssa_pa_t_kernel(tc, x_bytes, x_scale, freqs_cis, wq_a, wq_b, out_0, out
         for c in range(2, CHUNKS):
             load_x(c)
 
+
         ident = keep.tile([P, P], F32)
         make_identity(nc, ident[:])
         warm = keep.tile([P, 1], F32)
@@ -90,7 +92,15 @@ def tile_ssa_pa_t_kernel(tc, x_bytes, x_scale, freqs_cis, wq_a, wq_b, out_0, out
             nc.tensor.transpose(sb[:, t * P:(t + 1) * P], scale_col[:, t:t + 1].to_broadcast([P, P]), ident[:])
         nc.vector.tensor_copy(out=scale_row[:, 0:D].rearrange("p (n t) -> p n t", t=4),
                               in_=sb[:].rearrange("p (t n) -> p n t", t=4))
-        nc.scalar.copy(out=scale_row[:, D:2 * D], in_=scale_row[:, 0:D])
+        freq_rep = []
+        for g in range(G):
+            t = keep.tile([P, 512], F32, name="freq_rep%d" % g)
+            freq_rep.append(t)
+            words = freq_raw[:, g, :].bitcast(F32).rearrange("p (j a) -> p j a", j=J)
+            nc.scalar.copy(out=t[:].rearrange("p (j r a) -> p j r a", j=J, r=8),
+                           in_=words.unsqueeze(2).broadcast_to([P, J, 8, 16]))
+            if g == 0:
+                nc.scalar.copy(out=scale_row[:, D:2 * D], in_=scale_row[:, 0:D])
 
         wa_codes = keep.tile([P, 512], U32, align_bytes=64)
         wa_scales = keep.tile([P, 512], U8, align_bytes=64)
@@ -109,7 +119,7 @@ def tile_ssa_pa_t_kernel(tc, x_bytes, x_scale, freqs_cis, wq_a, wq_b, out_0, out
 
         def widen(u, half):
             c = UNITS[u][0]
-            t = work.tile([P, 2 * D], BF16, name="x_wide", tag="x_wide", bufs=4, align_bytes=64)
+            t = work.tile([P, 2 * D], BF16, name="x_wide", tag="x_wide", bufs=6, align_bytes=64)
             st["xw", c, half] = t
             src = x_raw[c][:, half * 2 * D:(half + 1) * 2 * D].bitcast(FP8)
             if u == 0:
@@ -126,7 +136,7 @@ def tile_ssa_pa_t_kernel(tc, x_bytes, x_scale, freqs_cis, wq_a, wq_b, out_0, out
                 st["xt", c, half] = b
                 turn_words(b, st["xw", c, half][:])
 
-        def grouprevx(u):
+        def group_x(u):
             c = UNITS[u][0]
             t = work.tile([P, 2048], BF16, name="x_grouped", tag="x_grouped", bufs=2, align_bytes=64)
             st["xg", u] = t
@@ -155,7 +165,7 @@ def tile_ssa_pa_t_kernel(tc, x_bytes, x_scale, freqs_cis, wq_a, wq_b, out_0, out
                 cols = slice(t * P, (t + 1) * P)
                 mx(b[:, cols], (wa_codes, wa_scales), cols, st["xq", u], slice(j * P, (j + 1) * P))
 
-        def grouprevq(u, j):
+        def group_q(u, j):
             if j >= UNITS[u][2]:
                 return
             if j == 0:
@@ -280,19 +290,12 @@ def tile_ssa_pa_t_kernel(tc, x_bytes, x_scale, freqs_cis, wq_a, wq_b, out_0, out
             dst = outs[a][b].rearrange("(g p j) h d -> p g (j h d)", p=P, j=J)[:, gs]
             nc.sync.dma_start(out=dst, in_=src)
 
-        def table_spread(g):
-            t = work.tile([P, 512], F32, name="freq_rep", tag="freq_rep", bufs=2)
-            st["frep", g] = t
-            words = freq_raw[:, g, :].bitcast(F32).rearrange("p (j a) -> p j a", j=J)
-            nc.scalar.copy(out=t[:].rearrange("p (j r a) -> p j r a", j=J, r=8),
-                           in_=words.unsqueeze(2).broadcast_to([P, J, 8, 16]))
-
         def table_turn(g):
             b = bank("n", 1)
             st["tb", g] = b
             for j in range(J):
                 cols = slice(j * P, (j + 1) * P)
-                nc.tensor.transpose(b[:, cols], st["frep", g][:, cols], ident[:])
+                nc.tensor.transpose(b[:, cols], freq_rep[g][:, cols], ident[:])
 
         def table_copy(g):
             t = keep.tile([P, 512], F32, name="table%d" % g)
@@ -305,25 +308,27 @@ def tile_ssa_pa_t_kernel(tc, x_bytes, x_scale, freqs_cis, wq_a, wq_b, out_0, out
         def live(u):
             return 0 <= u < NU
 
-        tail_stats = keep.tile([P, 2], F32)
-        tail_eta = keep.tile([P, 8], F32)
+        tail_stats = keep.tile([P, 4], F32)
+        tail_eta = {}
 
-        def tail_max(a):
-            lo = (G - 1) * 1024 + a * 512
-            nc.vector.tensor_reduce(out=tail_stats[:, a:a + 1], in_=st["res", last][:, lo:lo + 512],
+        def tail_max(a, half):
+            nc.vector.tensor_reduce(out=tail_stats[:, 2 * a + half:2 * a + half + 1], in_=res_of(NU - 2 + half, a),
                                     axis=AXIS_X, op=ALU.max)
 
-        def tail_turn(a):
-            t = bank("xt", 2)
-            st["tt", a] = t
-            nc.tensor.transpose(t[:, 0:P], tail_stats[:, a:a + 1].to_broadcast([P, P]), ident[:])
+        def direct_turn(key, cols, tag, bufs):
+            t = bank(tag, bufs)
+            st["tt", key] = t
+            for i in range(2):
+                nc.tensor.transpose(t[:, i * P:(i + 1) * P], cols[:, i:i + 1].to_broadcast([P, P]), ident[:])
 
-        def tail_step(a, i):
-            e = tail_eta[:, 4 * a:4 * a + 4]
+        def direct_step(key, w, i):
             if i == 0:
-                nc.vector.tensor_reduce(out=e[:, 0:1], in_=st["tt", a][:, 0:P], axis=AXIS_X, op=ALU.max)
+                tail_eta[key] = keep.tile([P, 4 * w], F32, name="tail_eta%s" % key)
+                nc.vector.tensor_reduce(out=tail_eta[key][:, 0:w],
+                                        in_=st["tt", key][:, 0:2 * P].rearrange("p (w n) -> p w n", w=w),
+                                        axis=AXIS_X, op=ALU.max)
             else:
-                eta_math(e, 1, i)
+                eta_math(tail_eta[key], w, i)
 
         def clamp_n(b, i, eng):
             a, h = divmod(i, H)
@@ -335,16 +340,22 @@ def tile_ssa_pa_t_kernel(tc, x_bytes, x_scale, freqs_cis, wq_a, wq_b, out_0, out
             b, i = divmod(s - 10, G)
             if s >= 10 and b < 2:
                 clamp_n(b, 2 * i + slot, "G" if G_CLAMP else "S")
-            if s == NU:
-                for i in range(2):
-                    clamp_n(2, 2 * slot + i, "G" if G_CLAMP else E2[2 * slot + i])
 
-        for s in range(NU + 1):
+        to_widen = [(u, half) for u in range(NU) for half in halves(u)]
+
+        def widen_slot(s, slot):
+            if to_widen and slot in WIDEN.get(s, (0, 1)):
+                widen(*to_widen.pop(0))
+
+        for s in range(NU):
             eb, ei = divmod(s - 9, G)
             eta_a = s >= 9 and ei == 0 and eb < last
             eta_b = s >= 9 and ei == 1 and eb < last
             if live(s - 3):
                 quantize("q", s - 3)
+            if eta_b:
+                eta_spread(eb)
+                eta_copy(eb)
             if live(s - 1):
                 turn_x(s - 1)
             if live(s - 4):
@@ -360,16 +371,11 @@ def tile_ssa_pa_t_kernel(tc, x_bytes, x_scale, freqs_cis, wq_a, wq_b, out_0, out
                 table_turn(TABLE_STEPS.index(s))
             if eta_a:
                 eta_turn(eb)
-            if eta_b:
-                eta_spread(eb)
             if live(s - 1):
-                grouprevx(s - 1)
-            if live(s):
-                widen(s, halves(s)[0])
+                group_x(s - 1)
+            widen_slot(s, 0)
             if eta_a:
                 eta_step(eb, 0)
-            if eta_b:
-                eta_copy(eb)
             if s == 1:
                 for i in range(2):
                     interleave_words(wa_grouped[:, i * 1024:(i + 1) * 1024], wab[i])
@@ -398,10 +404,9 @@ def tile_ssa_pa_t_kernel(tc, x_bytes, x_scale, freqs_cis, wq_a, wq_b, out_0, out
             if live(s - 3):
                 up(s - 3)
             if live(s - 2):
-                grouprevq(s - 2, 0)
-                grouprevq(s - 2, 1)
-            if live(s) and len(halves(s)) > 1:
-                widen(s, halves(s)[1])
+                group_q(s - 2, 0)
+                group_q(s - 2, 1)
+            widen_slot(s, 1)
             if eta_a:
                 eta_step(eb, 2)
             if live(s - 3):
@@ -411,79 +416,99 @@ def tile_ssa_pa_t_kernel(tc, x_bytes, x_scale, freqs_cis, wq_a, wq_b, out_0, out
                 down(s - 2, 3)
             if live(s - 3):
                 rope_a(s - 3)
-                rope_b(s - 3)
             if eta_a:
                 eta_step(eb, 3)
+            if live(s - 3):
+                rope_b(s - 3)
             if s == 1:
                 nc.vector.quantize_mx(out=wa_codes[:].bitcast(FP8X4), scales=wa_scales[:], in_=wa_grouped[:])
             if s == 2:
                 nc.vector.quantize_mx(out=wn_codes[:].bitcast(FP8X4), scales=wn_scales[:], in_=wn_grouped[:])
                 nc.vector.quantize_mx(out=wp_codes[:].bitcast(FP8X4), scales=wp_scales[:], in_=wp_grouped[:])
             if live(s - 2):
-                grouprevq(s - 2, 2)
-                grouprevq(s - 2, 3)
+                group_q(s - 2, 2)
+                group_q(s - 2, 3)
+            widen_slot(s, 2)
             if 1 <= s - 4 < NU - 2:
                 row_max(UNITS[s - 4][0])
             clamp_slot(s, 1)
-            if s + 1 in TABLE_STEPS:
-                table_spread(TABLE_STEPS.index(s + 1))
 
-        uprev, ua, ub = NU - 3, NU - 2, NU - 1
-        e2 = "GGGGGGGG" if G_CLAMP else E2
-        e3 = "GGGGGG" if G_CLAMP else E3
-        turn_p(uprev)
+        u14, u15, ua, ub = NU - 4, NU - 3, NU - 2, NU - 1
+        c13, c14 = CHUNKS - 3, CHUNKS - 2
+        quantize("q", u15)
+        eta_spread(2)
+        turn_x(ub)
+        eta_copy(2)
+        group_x(ub)
+        down(ua, 0)
+        down(ua, 1)
+        turn_p(u14)
+        clamp_n(2, 0, E2[0])
+        clamp_n(2, 1, E2[1])
+        quantize("x", ub)
+        up(u15)
+        group_q(ua, 0)
+        group_q(ua, 1)
         down(ub, 0)
         down(ub, 1)
+        silu_p(u14)
+        rope_a(u15)
+        rope_b(u15)
+        clamp_n(2, 2, E2[2])
+        clamp_n(2, 3, E2[3])
+        group_q(ub, 0)
+        group_q(ub, 1)
         quantize("q", ua)
-        silu_p(uprev)
-        grouprevq(ub, 0)
-        grouprevq(ub, 1)
+        turn_p(u15)
+        silu_n(u15)
         up(ua)
-        clamp_n(2, 4, e2[4])
-        clamp_n(2, 5, e2[5])
-        row_max(CHUNKS - 2)
-        eta_turn_at = bank("r", 1)
-        nc.tensor.transpose(eta_turn_at[:, 0:P], stats[:], ident[:])
-        st["eb", last] = eta_turn_at
+        row_max(c13)
         quantize("q", ub)
+        silu_p(u15)
+        clamp_n(2, 4, E2[4])
         up(ub)
+        clamp_n(2, 5, E2[5])
         silu_n(ua)
         silu_n(ub)
-        eta_step(last, 0)
+        row_max(c14)
+        eta_turn(last)
         rope_a(ua)
-        eta_step(last, 1)
+        clamp_n(2, 6, E2[6])
+        clamp_n(2, 7, E2[7])
+        eta_step(last, 0)
         rope_b(ua)
-        eta_step(last, 2)
         turn_p(ua)
-        rope_a(ub)
+        eta_step(last, 1)
+        tail_max(0, 0)
+        eta_step(last, 2)
+        tail_max(0, 1)
         eta_step(last, 3)
-        rope_b(ub)
+        direct_turn("a", tail_stats[:, 0:2], "xt", 2)
         eta_spread(last)
+        rope_a(ub)
+        rope_b(ub)
         turn_p(ub)
-        clamp_n(2, 6, e2[6])
-        clamp_n(2, 7, e2[7])
-        tail_max(0)
-        tail_turn(0)
         silu_p(ua)
         eta_copy(last)
+        direct_step("a", 1, 0)
+        tail_max(1, 0)
+        direct_step("a", 1, 1)
+        clamp(last, 0, 0, E3[0])
+        clamp(last, 0, 1, E3[1])
+        direct_step("a", 1, 2)
         silu_p(ub)
-        tail_step(0, 0)
-        clamp(last, 0, 0, e3[0])
-        tail_step(0, 1)
-        clamp(last, 0, 1, e3[1])
-        tail_max(1)
-        tail_turn(1)
-        tail_step(0, 2)
-        clamp(last, 0, 2, e3[2])
-        tail_step(0, 3)
-        tail_step(1, 0)
-        clamp(last, 0, 3, "V", col=tail_eta[:, 3:4])
+        clamp(last, 0, 2, E3[2])
+        direct_step("a", 1, 3)
+        tail_max(1, 1)
+        direct_turn("r", tail_stats[:, 2:4], "xt", 2)
+        clamp(last, 0, 3, "V", col=tail_eta["a"][:, 3:4])
         store(last, 0)
-        tail_step(1, 1)
-        clamp(last, 1, 0, e3[3])
-        tail_step(1, 2)
-        clamp(last, 1, 1, e3[4])
-        tail_step(1, 3)
-        clamp(last, 1, 2, e3[5])
-        clamp(last, 1, 3, "V", col=tail_eta[:, 7:8])
+        clamp(last, 1, 0, E3[3])
+        direct_step("r", 1, 0)
+        clamp(last, 1, 1, E3[4])
+        direct_step("r", 1, 1)
+        clamp(last, 1, 2, E3[5])
+        direct_step("r", 1, 2)
+        direct_step("r", 1, 3)
+        clamp(last, 1, 3, "V", col=tail_eta["r"][:, 3:4])
         store(last, 1)

from contextlib import ExitStack

import concourse.mybir as mybir
from concourse.masks import make_identity

B, S, D, H = 4, 2048, 512, 4
FLOPS = 2 * B * S * D * (512 + 256)

F32 = mybir.dt.float32
BF16 = mybir.dt.bfloat16
U32 = mybir.dt.uint32
U8 = mybir.dt.uint8
FP8 = mybir.dt.float8_e4m3fn
FP8X4 = mybir.dt.float8_e4m3fn_x4
ALU = mybir.AluOpType
ACT = mybir.ActivationFunctionType
AXIS_X = mybir.AxisListType.X

P = 128
G = 4
J = 4
CHUNKS = B * G
G_CLAMP = False
G_ROPE = False
E2 = "VVVVSSVS"
E3 = "SVSSSS"
WIDEN = {0: (0, 1), 1: (0, 1), 7: (0,), 8: (0,), 16: (0,), 17: (0,)}
TABLE_STEPS = [3, 5, 6, 7]
UNITS = [(0, 0, 2), (0, 2, 2)] + [(c, 0, J) for c in range(1, CHUNKS - 1)] + [(CHUNKS - 1, 0, 2), (CHUNKS - 1, 2, 2)]


def tile_ssa_pa_t_kernel(tc, x_bytes, x_scale, freqs_cis, wq_a, wq_b, out_0, out_1):
    nc = tc.nc
    outs = (out_0, out_1)

    with ExitStack() as ctx:
        keep = ctx.enter_context(tc.tile_pool(name="keep", bufs=1))
        work = ctx.enter_context(tc.tile_pool(name="work", bufs=3))
        psum = ctx.enter_context(tc.psum_pool(name="psum", bufs=1))
        ctx.enter_context(tc.manual_schedule())

        def bank(tag, bufs):
            return psum.tile([P, 512], F32, name=tag, tag=tag, bufs=bufs)

        scale_col = keep.tile([P, 4], F32)
        nc.sync.dma_start(out=scale_col[:], in_=x_scale.rearrange("a b (p t) -> p (a b t)", t=4))
        x_raw = []

        def load_x(c):
            t = keep.tile([P, J * D], U8, name="x_raw%d" % c, align_bytes=64)
            src = x_bytes[c // G].rearrange("(g p j) k -> g p (j k)", p=P, j=J)[c % G]
            nc.sync.dma_start(out=t[:], in_=src)
            x_raw.append(t)

        load_x(0)
        freq_raw = keep.tile([P, G, J * 32], BF16)
        nc.sync.dma_start(out=freq_raw[:], in_=freqs_cis.rearrange("(g p j) a e -> p g (j a e)", p=P, j=J))
        wa_raw = keep.tile([P, 4 * D], BF16)
        nc.sync.dma_start(out=wa_raw[:], in_=wq_a.rearrange("(m t) k -> m (t k)", t=4))
        load_x(1)
        wb_raw = keep.tile([P, 2 * D], BF16)
        nc.sync.dma_start(out=wb_raw[:], in_=wq_b.rearrange("(m e) k -> m (e k)", e=2))
        for c in range(2, CHUNKS):
            load_x(c)


        ident = keep.tile([P, P], F32)
        make_identity(nc, ident[:])
        warm = keep.tile([P, 1], F32)
        nc.scalar.activation(out=warm[:], in_=ident[:, 0:1], func=ACT.Silu)
        sign = keep.tile([P, 1], F32)
        nc.gpsimd.memset(sign[0:64, :], -1.0)
        nc.gpsimd.memset(sign[64:128, :], 1.0)
        stats = keep.tile([P, P], F32)
        nc.gpsimd.memset(stats[:], 0.0)

        def turn_words(dst_bank, src_bf16):
            words = src_bf16.bitcast(F32)
            for j in range(2):
                for u in range(2):
                    q = 2 * j + u
                    nc.tensor.transpose(dst_bank[:, q * P:(q + 1) * P],
                                        words[:, 256 * j + u:256 * (j + 1):2], ident[:])

        def interleave_words(dst_bf16, src_bank):
            nc.scalar.copy(out=dst_bf16.bitcast(F32).rearrange("p (j r u) -> p j r u", j=2, u=2),
                           in_=src_bank[:].rearrange("p (j u r) -> p j r u", j=2, u=2))

        scale_row = keep.tile([P, 2 * D], F32)
        sb = bank("n", 1)
        for t in range(4):
            nc.tensor.transpose(sb[:, t * P:(t + 1) * P], scale_col[:, t:t + 1].to_broadcast([P, P]), ident[:])
        nc.vector.tensor_copy(out=scale_row[:, 0:D].rearrange("p (n t) -> p n t", t=4),
                              in_=sb[:].rearrange("p (t n) -> p n t", t=4))
        freq_rep = []
        for g in range(G):
            t = keep.tile([P, 512], F32, name="freq_rep%d" % g)
            freq_rep.append(t)
            words = freq_raw[:, g, :].bitcast(F32).rearrange("p (j a) -> p j a", j=J)
            nc.scalar.copy(out=t[:].rearrange("p (j r a) -> p j r a", j=J, r=8),
                           in_=words.unsqueeze(2).broadcast_to([P, J, 8, 16]))
            if g == 0:
                nc.scalar.copy(out=scale_row[:, D:2 * D], in_=scale_row[:, 0:D])

        wa_codes = keep.tile([P, 512], U32, align_bytes=64)
        wa_scales = keep.tile([P, 512], U8, align_bytes=64)
        wa_grouped = keep.tile([P, 2048], BF16, align_bytes=64)
        wn_codes = keep.tile([P, 128], U32, align_bytes=64)
        wn_scales = keep.tile([P, 128], U8, align_bytes=64)
        wn_grouped = keep.tile([P, 512], BF16, align_bytes=64)
        wp_codes = keep.tile([P, 256], U32, align_bytes=64)
        wp_scales = keep.tile([P, 256], U8, align_bytes=64)
        wp_grouped = keep.tile([P, 1024], BF16, align_bytes=64)

        st = {}

        def halves(u):
            return range(UNITS[u][1] // 2, (UNITS[u][1] + UNITS[u][2]) // 2)

        def widen(u, half):
            c = UNITS[u][0]
            t = work.tile([P, 2 * D], BF16, name="x_wide", tag="x_wide", bufs=6, align_bytes=64)
            st["xw", c, half] = t
            src = x_raw[c][:, half * 2 * D:(half + 1) * 2 * D].bitcast(FP8)
            if u == 0:
                for j in range(2):
                    nc.vector.tensor_tensor(out=t[:, j * D:(j + 1) * D], in0=src[:, j * D:(j + 1) * D],
                                            in1=scale_row[:, 0:D], op=ALU.mult)
            else:
                nc.vector.tensor_tensor(out=t[:], in0=src, in1=scale_row[:], op=ALU.mult)

        def turn_x(u):
            c = UNITS[u][0]
            for half in halves(u):
                b = bank("xt", 2)
                st["xt", c, half] = b
                turn_words(b, st["xw", c, half][:])

        def group_x(u):
            c = UNITS[u][0]
            t = work.tile([P, 2048], BF16, name="x_grouped", tag="x_grouped", bufs=2, align_bytes=64)
            st["xg", u] = t
            for i, half in enumerate(halves(u)):
                interleave_words(t[:, i * 1024:(i + 1) * 1024], st["xt", c, half])

        def quantize(kind, u):
            n = UNITS[u][2] * P
            codes = work.tile([P, 512], U32, name=kind + "_codes", tag=kind + "_codes", bufs=3, align_bytes=64)
            scales = work.tile([P, 512], U8, name=kind + "_scales", tag=kind + "_scales", bufs=3, align_bytes=64)
            st[kind + "q", u] = (codes, scales)
            nc.vector.quantize_mx(out=codes[:, 0:n].bitcast(FP8X4), scales=scales[:, 0:n],
                                  in_=st[kind + "g", u][:, 0:4 * n])

        def mx(out, lhs, lcols, rhs, rcols):
            nc.tensor.matmul_mx(out=out, lhsT=lhs[0][:, lcols].bitcast(FP8X4), lhsT_scale=lhs[1][:, lcols],
                                rhs=rhs[0][:, rcols].bitcast(FP8X4), rhs_scale=rhs[1][:, rcols],
                                start=True, stop=True)

        def down(u, j):
            if j >= UNITS[u][2]:
                return
            b = bank("qc", 2)
            st["qcb", u, j] = b
            for t in range(4):
                cols = slice(t * P, (t + 1) * P)
                mx(b[:, cols], (wa_codes, wa_scales), cols, st["xq", u], slice(j * P, (j + 1) * P))

        def group_q(u, j):
            if j >= UNITS[u][2]:
                return
            if j == 0:
                st["qg", u] = work.tile([P, 2048], BF16, name="q_grouped", tag="q_grouped", bufs=2, align_bytes=64)
            nc.scalar.copy(out=st["qg", u][:, j * 512:(j + 1) * 512].rearrange("p (n t) -> p n t", t=4),
                           in_=st["qcb", u, j][:].rearrange("p (t n) -> p n t", t=4))

        def up(u):
            n = UNITS[u][2] * P
            for r in range(2):
                if r == 0 or n == 512:
                    b = bank("pp", 2)
                lo = 0 if n == 512 else r * n
                st["pp", u, r] = b[:, lo:lo + n]
                mx(st["pp", u, r], (wp_codes, wp_scales), slice(64 * r, 64 * r + P), st["qq", u], slice(0, n))
            b = bank("xt", 2) if u == len(UNITS) - 1 else bank("n", 1)
            st["n", u] = b
            for j in range(UNITS[u][2]):
                cols = slice(j * P, (j + 1) * P)
                mx(b[:, cols], st["qq", u], cols, (wn_codes, wn_scales), slice(0, P))

        def res_of(u, a):
            c, j0, nj = UNITS[u]
            if ("res", c // G) not in st:
                st["res", c // G] = work.tile([P, G * 1024], F32, name="res", tag="res", bufs=3)
            lo = (c % G) * 1024 + a * 512 + j0 * P
            return st["res", c // G][:, lo:lo + nj * P]

        def silu_n(u):
            n = UNITS[u][2] * P
            nc.scalar.activation(out=res_of(u, 0), in_=st["n", u][:, 0:n], func=ACT.Silu)

        def rope_table(u):
            c, j0, nj = UNITS[u]
            return st["tab", c % G][:, j0 * P:(j0 + nj) * P].bitcast(BF16).rearrange("p (n e) -> p n e", e=2)

        def rope_a(u):
            n = UNITS[u][2] * P
            ta = work.tile([P, 512], F32, name="rope_a", tag="rope_a", bufs=2)
            st["ra", u] = ta
            nc.vector.tensor_tensor(out=ta[:, 0:n], in0=st["pp", u, 0], in1=rope_table(u)[:, :, 0], op=ALU.mult)

        def rope_b(u):
            n = UNITS[u][2] * P
            tb = work.tile([P, 512], F32, name="rope_b", tag="rope_b", bufs=2)
            st["rb", u] = tb
            if G_ROPE and u < len(UNITS) - 2:
                tcopy = work.tile([P, 512], F32, name="rope_c", tag="rope_c", bufs=2)
                nc.scalar.activation(out=tcopy[:, 0:n], in_=st["pp", u, 1], func=ACT.Copy, scale=sign[:])
                nc.gpsimd.tensor_tensor(out=tb[:, 0:n], in0=tcopy[:, 0:n], in1=rope_table(u)[:, :, 1], op=ALU.mult)
            else:
                nc.vector.scalar_tensor_tensor(out=tb[:, 0:n], in0=st["pp", u, 1], scalar=sign[:],
                                               in1=rope_table(u)[:, :, 1], op0=ALU.mult, op1=ALU.mult)

        def turn_p(u):
            b = bank("qc", 2) if u == len(UNITS) - 1 else bank("r", 1)
            st["r", u] = b
            for j in range(UNITS[u][2]):
                cols = slice(j * P, (j + 1) * P)
                for i, k in enumerate(("ra", "rb")):
                    nc.tensor.matmul(out=b[:, cols], lhsT=st[k, u][:, cols], rhs=ident[:],
                                     is_transpose=True, start=(i == 0), stop=(i == 1))

        def silu_p(u):
            nj = UNITS[u][2]
            nc.scalar.activation(
                out=res_of(u, 1).rearrange("p (j f e) -> p j f e", j=nj, e=2),
                in_=st["r", u][:, 0:nj * P].rearrange("p (j e f) -> p j f e", j=nj, e=2), func=ACT.Silu)

        def row_max(c):
            g = c % G
            nc.vector.tensor_reduce(
                out=stats[:, 2 * c:2 * c + 2],
                in_=st["res", c // G][:, g * 1024:(g + 1) * 1024].rearrange("p (a n) -> p a n", a=2),
                axis=AXIS_X, op=ALU.max)

        def eta_math(e, w, i):
            if i == 1:
                nc.vector.scalar_tensor_tensor(out=e[:, w:2 * w], in0=e[:, 0:w], scalar=0.0, in1=e[:, 0:w],
                                               op0=ALU.is_equal, op1=ALU.add)
            elif i == 2:
                nc.vector.reciprocal(out=e[:, 2 * w:3 * w], in_=e[:, w:2 * w])
            else:
                nc.vector.tensor_scalar(out=e[:, 3 * w:4 * w], in0=e[:, 2 * w:3 * w], scalar1=10.0, scalar2=1.0,
                                        op0=ALU.mult, op1=ALU.min)

        def eta_turn(b):
            t = bank("n", 1)
            st["eb", b] = t
            nc.tensor.transpose(t[:, 0:P], stats[:], ident[:])

        def eta_step(b, i):
            if i == 0:
                st["e", b] = work.tile([P, 4], F32, name="eta_col", tag="eta_col", bufs=2)
                nc.vector.tensor_reduce(out=st["e", b][:, 0:1], in_=st["eb", b][:, 0:P], axis=AXIS_X, op=ALU.max)
            else:
                eta_math(st["e", b], 1, i)

        def eta_spread(b):
            t = bank("n", 1)
            st["es", b] = t
            nc.tensor.transpose(t[:, 0:P], st["e", b][:, 3:4].to_broadcast([P, P]), ident[:])

        def eta_copy(b):
            t = work.tile([P, 8], F32, name="eta_row", tag="eta_row", bufs=2)
            st["eta", b] = t
            nc.scalar.copy(out=t[:], in_=st["es", b][:, 8 * b:8 * b + 8])

        def clamp(b, a, h, eng, gs=slice(0, G), col=None):
            v = st["res", b][:].rearrange("p (g a j h d) -> p a h g j d", g=G, a=2, j=J, h=H)[:, a, h, gs]
            if col is None:
                col = st["eta", b][:, 2 * h + a:2 * h + a + 1]
            if eng == "V":
                nc.vector.tensor_scalar(out=v, in0=v, scalar1=col, scalar2=None, op0=ALU.mult)
            elif eng == "G":
                nc.gpsimd.tensor_scalar(out=v, in0=v, scalar1=col, scalar2=0.0, op0=ALU.mult, op1=ALU.add)
            else:
                nc.scalar.activation(out=v, in_=v, func=ACT.Copy, scale=col)

        def store(b, a, gs=slice(0, G)):
            src = st["res", b][:].rearrange("p (g a n) -> p a g n", g=G, a=2)[:, a, gs]
            dst = outs[a][b].rearrange("(g p j) h d -> p g (j h d)", p=P, j=J)[:, gs]
            nc.sync.dma_start(out=dst, in_=src)

        def table_turn(g):
            b = bank("n", 1)
            st["tb", g] = b
            for j in range(J):
                cols = slice(j * P, (j + 1) * P)
                nc.tensor.transpose(b[:, cols], freq_rep[g][:, cols], ident[:])

        def table_copy(g):
            t = keep.tile([P, 512], F32, name="table%d" % g)
            st["tab", g] = t
            nc.scalar.copy(out=t[:], in_=st["tb", g][:])

        NU = len(UNITS)
        last = B - 1

        def live(u):
            return 0 <= u < NU

        tail_stats = keep.tile([P, 4], F32)
        tail_eta = {}

        def tail_max(a, half):
            nc.vector.tensor_reduce(out=tail_stats[:, 2 * a + half:2 * a + half + 1], in_=res_of(NU - 2 + half, a),
                                    axis=AXIS_X, op=ALU.max)

        def direct_turn(key, cols, tag, bufs):
            t = bank(tag, bufs)
            st["tt", key] = t
            for i in range(2):
                nc.tensor.transpose(t[:, i * P:(i + 1) * P], cols[:, i:i + 1].to_broadcast([P, P]), ident[:])

        def direct_step(key, w, i):
            if i == 0:
                tail_eta[key] = keep.tile([P, 4 * w], F32, name="tail_eta%s" % key)
                nc.vector.tensor_reduce(out=tail_eta[key][:, 0:w],
                                        in_=st["tt", key][:, 0:2 * P].rearrange("p (w n) -> p w n", w=w),
                                        axis=AXIS_X, op=ALU.max)
            else:
                eta_math(tail_eta[key], w, i)

        def clamp_n(b, i, eng):
            a, h = divmod(i, H)
            clamp(b, a, h, eng)
            if h == H - 1:
                store(b, a)

        def clamp_slot(s, slot):
            b, i = divmod(s - 10, G)
            if s >= 10 and b < 2:
                clamp_n(b, 2 * i + slot, "G" if G_CLAMP else "S")

        to_widen = [(u, half) for u in range(NU) for half in halves(u)]

        def widen_slot(s, slot):
            if to_widen and slot in WIDEN.get(s, (0, 1)):
                widen(*to_widen.pop(0))

        for s in range(NU):
            eb, ei = divmod(s - 9, G)
            eta_a = s >= 9 and ei == 0 and eb < last
            eta_b = s >= 9 and ei == 1 and eb < last
            if live(s - 3):
                quantize("q", s - 3)
            if eta_b:
                eta_spread(eb)
                eta_copy(eb)
            if live(s - 1):
                turn_x(s - 1)
            if live(s - 4):
                turn_p(s - 4)
            if s == 1:
                wab = [bank("pp", 2), bank("pp", 2)]
                for i in range(2):
                    turn_words(wab[i], wa_raw[:, i * 1024:(i + 1) * 1024])
            if s == 2:
                wbb = bank("r", 1)
                turn_words(wbb, wb_raw[:])
            if s in TABLE_STEPS:
                table_turn(TABLE_STEPS.index(s))
            if eta_a:
                eta_turn(eb)
            if live(s - 1):
                group_x(s - 1)
            widen_slot(s, 0)
            if eta_a:
                eta_step(eb, 0)
            if s == 1:
                for i in range(2):
                    interleave_words(wa_grouped[:, i * 1024:(i + 1) * 1024], wab[i])
            if s == 2:
                src = wbb[:].rearrange("p (e u h f j) -> p f h j e u", e=2, u=2, h=H, f=2)
                nc.scalar.copy(out=wn_grouped[:].bitcast(F32).rearrange("p (h j e u) -> p h j e u", h=H, e=2, u=2),
                               in_=src[:, 0])
                srcp = wbb[:].rearrange("p (e u h f j) -> p f e h j u", e=2, u=2, h=H, f=2)
                for r in range(2):
                    nc.scalar.copy(
                        out=wp_grouped[:, r * 512:(r + 1) * 512].bitcast(F32).rearrange(
                            "p (e h j u) -> p e h j u", e=2, h=H, u=2),
                        in_=srcp[:, 1])
            if s in TABLE_STEPS:
                table_copy(TABLE_STEPS.index(s))
            clamp_slot(s, 0)
            if live(s - 4):
                silu_p(s - 4)
            if live(s - 1):
                quantize("x", s - 1)
            if eta_a:
                eta_step(eb, 1)
            if live(s - 2):
                down(s - 2, 0)
                down(s - 2, 1)
            if live(s - 3):
                up(s - 3)
            if live(s - 2):
                group_q(s - 2, 0)
                group_q(s - 2, 1)
            widen_slot(s, 1)
            if eta_a:
                eta_step(eb, 2)
            if live(s - 3):
                silu_n(s - 3)
            if live(s - 2):
                down(s - 2, 2)
                down(s - 2, 3)
            if live(s - 3):
                rope_a(s - 3)
            if eta_a:
                eta_step(eb, 3)
            if live(s - 3):
                rope_b(s - 3)
            if s == 1:
                nc.vector.quantize_mx(out=wa_codes[:].bitcast(FP8X4), scales=wa_scales[:], in_=wa_grouped[:])
            if s == 2:
                nc.vector.quantize_mx(out=wn_codes[:].bitcast(FP8X4), scales=wn_scales[:], in_=wn_grouped[:])
                nc.vector.quantize_mx(out=wp_codes[:].bitcast(FP8X4), scales=wp_scales[:], in_=wp_grouped[:])
            if live(s - 2):
                group_q(s - 2, 2)
                group_q(s - 2, 3)
            widen_slot(s, 2)
            if 1 <= s - 4 < NU - 2:
                row_max(UNITS[s - 4][0])
            clamp_slot(s, 1)

        u14, u15, ua, ub = NU - 4, NU - 3, NU - 2, NU - 1
        c13, c14 = CHUNKS - 3, CHUNKS - 2
        quantize("q", u15)
        eta_spread(2)
        turn_x(ub)
        eta_copy(2)
        group_x(ub)
        down(ua, 0)
        down(ua, 1)
        turn_p(u14)
        clamp_n(2, 0, E2[0])
        clamp_n(2, 1, E2[1])
        quantize("x", ub)
        up(u15)
        group_q(ua, 0)
        group_q(ua, 1)
        down(ub, 0)
        down(ub, 1)
        silu_p(u14)
        rope_a(u15)
        rope_b(u15)
        clamp_n(2, 2, E2[2])
        clamp_n(2, 3, E2[3])
        group_q(ub, 0)
        group_q(ub, 1)
        quantize("q", ua)
        turn_p(u15)
        silu_n(u15)
        up(ua)
        row_max(c13)
        quantize("q", ub)
        silu_p(u15)
        clamp_n(2, 4, E2[4])
        up(ub)
        clamp_n(2, 5, E2[5])
        silu_n(ua)
        silu_n(ub)
        row_max(c14)
        eta_turn(last)
        rope_a(ua)
        clamp_n(2, 6, E2[6])
        clamp_n(2, 7, E2[7])
        eta_step(last, 0)
        rope_b(ua)
        turn_p(ua)
        eta_step(last, 1)
        tail_max(0, 0)
        eta_step(last, 2)
        tail_max(0, 1)
        eta_step(last, 3)
        direct_turn("a", tail_stats[:, 0:2], "xt", 2)
        eta_spread(last)
        rope_a(ub)
        rope_b(ub)
        turn_p(ub)
        silu_p(ua)
        eta_copy(last)
        direct_step("a", 1, 0)
        tail_max(1, 0)
        direct_step("a", 1, 1)
        clamp(last, 0, 0, E3[0])
        clamp(last, 0, 1, E3[1])
        direct_step("a", 1, 2)
        silu_p(ub)
        clamp(last, 0, 2, E3[2])
        direct_step("a", 1, 3)
        tail_max(1, 1)
        direct_turn("r", tail_stats[:, 2:4], "xt", 2)
        clamp(last, 0, 3, "V", col=tail_eta["a"][:, 3:4])
        store(last, 0)
        clamp(last, 1, 0, E3[3])
        direct_step("r", 1, 0)
        clamp(last, 1, 1, E3[4])
        direct_step("r", 1, 1)
        clamp(last, 1, 2, E3[5])
        direct_step("r", 1, 2)
        direct_step("r", 1, 3)
        clamp(last, 1, 3, "V", col=tail_eta["r"][:, 3:4])
        store(last, 1)
